import numpy as np
import ml_dtypes


def mxq(x, axis, fmt="e4m3"):
    dtype, down = {"e4m3": (ml_dtypes.float8_e4m3fn, 7), "e5m2": (ml_dtypes.float8_e5m2, 14)}[fmt]
    v = np.moveaxis(np.asarray(x, np.float32).astype(ml_dtypes.bfloat16).astype(np.float64), axis, -1)
    blocks = v.reshape(v.shape[:-1] + (-1, 32))
    amax = np.abs(blocks).max(-1, keepdims=True)
    byte = np.maximum(np.where(amax > 0, np.frexp(amax)[1] - 1 + 127, 0) - down, 1)
    scale = np.exp2(byte - 127.0)
    codes = (blocks / scale).astype(np.float32).astype(dtype).astype(np.float64)
    return np.moveaxis((codes * scale).reshape(v.shape), -1, axis)


WIDE = False


def mx_kscale(k):
    if not WIDE:
        return np.ones(k)
    levels = np.array([10, -10, 5, -5, 0])
    if k % 512:
        return np.exp2(np.random.permutation(np.resize(levels, k // 32))).repeat(32)
    a = np.empty((k // 512, 16))
    for p in range(k // 512):
        a[p, :8] = np.random.permutation(np.resize(levels, 8))
        for g in range(8):
            far = levels[np.abs(levels - a[p, g]) >= 10]
            a[p, g + 8] = far[np.random.randint(len(far))]
    return np.exp2(a.ravel()).repeat(32)


BF16 = ml_dtypes.bfloat16


def bf(x):
    return np.asarray(x, np.float32).astype(BF16)


def f64(x):
    return np.asarray(x).astype(np.float64)


M, N, H = 4096, 512, 512
RMIN, RMAX = 0.4, 0.99


def half_glorot(rows, cols):
    limit = np.sqrt(1.5 / ((rows + cols) / 2.0))
    return np.random.uniform(-limit, limit, (rows, cols))


def setup_inputs():
    s, t = mx_kscale(N), mx_kscale(H)
    inputs = np.random.standard_normal((M, N))
    state_re = np.random.standard_normal((M, H))
    state_im = np.random.standard_normal((M, H))
    C_re = half_glorot(H, N)
    C_im = half_glorot(H, N)
    B_re = half_glorot(N, H)
    B_im = half_glorot(N, H)
    D = np.random.standard_normal(N)
    nu = np.random.uniform(np.log(-np.log(RMAX)), np.log(-np.log(RMIN)), H)
    theta = np.random.uniform(0.0, 3.14 / 10, H)
    gamma = np.sqrt(1.0 - np.exp(-2.0 * np.exp(nu)))
    return {"inputs": bf(inputs * s), "state_re": bf(state_re * t), "state_im": bf(state_im * t),
            "B_re": bf(B_re / s[:, None]), "B_im": bf(B_im / s[:, None]),
            "C_re": bf(C_re / t[:, None]), "C_im": bf(C_im / t[:, None]),
            "D": bf(D / s), "nu": bf(nu), "theta": bf(theta), "gamma": bf(gamma * t)}


def reference(inputs, state_re, state_im, B_re, B_im, C_re, C_im, D, nu, theta, gamma):
    u = f64(inputs)
    mag = np.exp(-np.exp(f64(nu)))
    lam_re = mag * np.cos(f64(theta))
    lam_im = mag * np.sin(f64(theta))
    uq = mxq(u, 1, "e4m3")
    new_u_re = f64(gamma) * (uq @ mxq(f64(B_re), 0, "e4m3"))
    new_u_im = f64(gamma) * (uq @ mxq(f64(B_im), 0, "e4m3"))
    x_re = f64(state_re) * lam_re - f64(state_im) * lam_im + new_u_re
    x_im = f64(state_re) * lam_im + f64(state_im) * lam_re + new_u_im
    y = (mxq(x_re, 1, "e4m3") @ mxq(f64(C_re), 0, "e4m3")) - (mxq(x_im, 1, "e4m3") @ mxq(f64(C_im), 0, "e4m3")) + f64(D) * u
    return y, x_re, x_im

@@ -1,0 +1,426 @@
+from contextlib import ExitStack
+import math
+
+import concourse.mybir as mybir
+from concourse.masks import make_identity
+
+F32 = mybir.dt.float32
+BF16 = mybir.dt.bfloat16
+U32 = mybir.dt.uint32
+U8 = mybir.dt.uint8
+I32 = mybir.dt.int32
+FP8X4 = mybir.dt.float8_e4m3fn_x4
+ALU = mybir.AluOpType
+ACTF = mybir.ActivationFunctionType
+
+P = 128
+ROWS = 4096
+WIDTH = 512
+FLOPS = 4 * 2 * ROWS * WIDTH * WIDTH
+
+TWO_PI_HI = 6.28125
+TWO_PI_LO = 2.0 * math.pi - 6.28125
+CHUNKS = [512] * 7 + [256, 256]
+
+NCH = len(CHUNKS)
+NPL = 4 * NCH
+OFFS = [sum(CHUNKS[:c]) for c in range(NCH)]
+assert sum(CHUNKS) == ROWS
+YLAG = 7
+Y_OFF = -1
+KQ = 2
+
+
+def tile_linearrecurrentunitcell_t_kernel(
+    tc, inputs, state_re, state_im, B_re, B_im, C_re, C_im, D, nu, theta, gamma, out_0, out_1, out_2
+):
+    nc = tc.nc
+    with ExitStack() as ctx:
+        ctx.enter_context(tc.manual_schedule())
+        const = ctx.enter_context(tc.tile_pool(name="const", bufs=1))
+        io = ctx.enter_context(tc.tile_pool(name="io", bufs=3))
+        work = ctx.enter_context(tc.tile_pool(name="work", bufs=2))
+        psum = ctx.enter_context(tc.psum_pool(name="psum", bufs=1))
+
+        def ok(c):
+            return 0 <= c < NCH
+
+        def okp(g):
+            return 0 <= g < NPL
+
+        def rows(c):
+            return CHUNKS[c]
+
+        def mt(c):
+            return CHUNKS[c] // P
+
+        pr_nu = const.tile([P, 4], BF16, name="pr_nu")
+        pr_th = const.tile([P, 4], BF16, name="pr_th")
+        pr_ga = const.tile([P, 4], BF16, name="pr_ga")
+        with nc.allow_non_contiguous_dma(reason="three vectors of 512 values, four neighbours a piece"):
+            for dst, vec in ((pr_nu, nu), (pr_th, theta), (pr_ga, gamma)):
+                nc.scalar.dma_start(
+                    out=dst[:], in_=vec.rearrange("(p t) -> p t", t=4),
+                )
+        dbc = const.tile([P, WIDTH], BF16, name="dbc")
+        nc.scalar.dma_start(out=dbc[:], in_=D.partition_broadcast(P))
+
+        u_t = {}
+        sre_t = {}
+        sim_t = {}
+
+        def rows_of(dram, c):
+            return dram[OFFS[c]:OFFS[c] + rows(c), :]
+
+        def load_u(c):
+            u_sb = io.tile([P, mt(c) * WIDTH], BF16, tag="u", name="u_sb", bufs=4)
+            nc.sync.dma_start(out=u_sb[:], in_=rows_of(inputs, c).rearrange("(i j) k -> i (j k)", j=mt(c)))
+            u_t[c] = u_sb
+
+        def load_s(c):
+            sre = io.tile([P, mt(c) * WIDTH], BF16, tag="sre", name="sre")
+            nc.sync.dma_start(out=sre[:], in_=rows_of(state_re, c).rearrange("(i j) k -> i (j k)", j=mt(c)))
+            sre_t[c] = sre
+            sim = io.tile([P, mt(c) * WIDTH], BF16, tag="sim", name="sim")
+            nc.sync.dma_start(out=sim[:], in_=rows_of(state_im, c).rearrange("(i j) k -> i (j k)", j=mt(c)))
+            sim_t[c] = sim
+
+        def load_w(w, nm, tg):
+            raw = work.tile([P, 4 * WIDTH], BF16, tag=tg, name="raw_" + nm)
+            nc.sync.dma_start(
+                out=raw[:], in_=w.rearrange("(p t) c -> p (t c)", t=4),
+            )
+            return raw
+
+        raw_bre = load_w(B_re, "bre", "xore")
+        raw_bim = load_w(B_im, "bim", "xore")
+        load_u(0)
+        load_s(0)
+        load_u(1)
+        raw_cre = load_w(C_re, "cre", "xoim")
+        raw_cim = load_w(C_im, "cim", "xoim")
+        load_s(1)
+        load_u(2)
+        load_s(2)
+        load_u(3)
+
+        ident = const.tile([P, P], F32, name="ident")
+        make_identity(nc, ident[:])
+
+        def small(nm, dt=F32):
+            return const.tile([P, 4], dt, name=nm)
+
+        def quant(g_ap, nm):
+            cd = const.tile([P, WIDTH], U32, name="cd_" + nm, align_bytes=64)
+            sc = const.tile([P, WIDTH], U8, name="sc_" + nm, align_bytes=64)
+            nc.vector.quantize_mx(out=cd[:].bitcast(FP8X4), scales=sc[:], in_=g_ap)
+            return cd, sc
+
+        def regroup_b(raw, nm):
+            g = work.tile([P, 4 * WIDTH], BF16, tag="gxre", name="g_" + nm, align_bytes=64)
+            src = raw[:].rearrange("p (t q s) -> p s q t", t=4, s=4)
+            dst = g[:].rearrange("p (s q t) -> p s q t", s=4, t=4)
+            for half in range(2):
+                nc.vector.tensor_copy(out=dst[:, 2 * half:2 * half + 2], in_=src[:, 2 * half:2 * half + 2])
+            return g
+
+        thf = small("thf")
+        nc.vector.tensor_copy(out=thf[:], in_=pr_th[:])
+        kq = small("kq")
+        nc.vector.tensor_scalar_mul(out=kq[:], in0=thf[:], scalar1=1.0 / (2.0 * math.pi))
+        ki = small("ki", I32)
+        nc.vector.tensor_copy(out=ki[:], in_=kq[:])
+        kf = small("kf")
+        nc.vector.tensor_copy(out=kf[:], in_=ki[:])
+        r1 = small("r1")
+        nc.vector.scalar_tensor_tensor(out=r1[:], in0=kf[:], scalar=-TWO_PI_HI, in1=thf[:], op0=ALU.mult, op1=ALU.add)
+        r2 = small("r2")
+        nc.vector.scalar_tensor_tensor(out=r2[:], in0=kf[:], scalar=-TWO_PI_LO, in1=r1[:], op0=ALU.mult, op1=ALU.add)
+        gam = small("gam")
+        nc.vector.tensor_copy(out=gam[:], in_=pr_ga[:])
+        e1 = small("e1")
+        nc.scalar.activation(out=e1[:], in_=pr_nu[:], func=ACTF.Exp)
+        mag = small("mag")
+        nc.scalar.activation(out=mag[:], in_=e1[:], func=ACTF.Exp, scale=-1.0)
+        sa = small("sa")
+        nc.scalar.activation(out=sa[:], in_=r2[:], func=ACTF.Sin, scale=0.5)
+        sb = small("sb")
+        nc.scalar.activation(out=sb[:], in_=r2[:], func=ACTF.Sin, scale=0.25)
+
+        g_bre = regroup_b(raw_bre, "bre")
+        g_bim = regroup_b(raw_bim, "bim")
+
+        sa2 = small("sa2")
+        nc.vector.tensor_tensor(out=sa2[:], in0=sa[:], in1=sa[:], op=ALU.mult)
+        cosr = small("cosr")
+        nc.vector.tensor_scalar(out=cosr[:], in0=sa2[:], scalar1=-2.0, scalar2=1.0, op0=ALU.mult, op1=ALU.add)
+        sb2 = small("sb2")
+        nc.vector.tensor_tensor(out=sb2[:], in0=sb[:], in1=sb[:], op=ALU.mult)
+        ch2 = small("ch2")
+        nc.vector.tensor_scalar(out=ch2[:], in0=sb2[:], scalar1=-4.0, scalar2=2.0, op0=ALU.mult, op1=ALU.add)
+        sinr = small("sinr")
+        nc.vector.tensor_tensor(out=sinr[:], in0=sa[:], in1=ch2[:], op=ALU.mult)
+        lam_re = small("lam_re")
+        nc.vector.tensor_tensor(out=lam_re[:], in0=mag[:], in1=cosr[:], op=ALU.mult)
+        lam_im = small("lam_im")
+        nc.vector.tensor_tensor(out=lam_im[:], in0=mag[:], in1=sinr[:], op=ALU.mult)
+        nlam_im = small("nlam_im")
+        nc.vector.tensor_scalar_mul(out=nlam_im[:], in0=lam_im[:], scalar1=-1.0)
+
+        b_cd = [quant(g_bre[:], "bre"), quant(g_bim[:], "bim")]
+        c_cd = []
+
+        gu_t = {}
+        ut_t = {}
+        uq_t = {}
+        du_t = {}
+        xT_t = {}
+        gx_t = {}
+        xq_t = {}
+        xo_t = {}
+        yo_t = {}
+        st_t = {}
+        pp_t = {}
+        xn_t = {}
+        yy_t = {}
+
+        gu_t[1] = work.tile([P, 4 * rows(1)], BF16, tag="du", name="gu1", align_bytes=64)
+        g_c = work.tile([P, 2, 4 * WIDTH], BF16, tag="du", name="g_c", align_bytes=64)
+        for ri, (raw, sign) in enumerate(((raw_cre, 1.0), (raw_cim, -1.0))):
+            nc.gpsimd.tensor_scalar(
+                out=g_c[:, ri, :].rearrange("p (n t) -> p n t", t=4),
+                in0=raw[:].rearrange("p (t n) -> p n t", t=4),
+                scalar1=sign, scalar2=0.0, op0=ALU.mult, op1=ALU.add,
+            )
+
+        def pe_ut(c, hc):
+            u_w = u_t[c][:].bitcast(F32)
+            ut = psum.tile([P, 2, 256], F32, tag="ut", name="ut")
+            for jj in range(2):
+                j = 2 * hc + jj
+                for u in range(2):
+                    nc.tensor.transpose(
+                        ut[:, u, jj * P:(jj + 1) * P], u_w[:, j * 256 + u:(j + 1) * 256:2], ident[:]
+                    )
+            ut_t[(c, hc)] = ut
+
+        def pe_st(c, u, which):
+            src_t, tg = ((sre_t, "str"), (sim_t, "sti"))[which]
+            s_w = src_t[c][:].bitcast(F32)
+            st = psum.tile([P, rows(c)], F32, tag=tg, name=tg)
+            for j in range(mt(c)):
+                nc.tensor.transpose(st[:, j * P:(j + 1) * P], s_w[:, j * 256 + u:(j + 1) * 256:2], ident[:])
+            st_t[(c, u, which)] = st[:].bitcast(BF16).rearrange("p (m e) -> p m e", e=2)
+
+        def pe_m1(g):
+            c, t = divmod(g, 4)
+            uc, us = uq_t[c]
+            for ri in range(2):
+                cd, sc = b_cd[ri]
+                pp = psum.tile([P, rows(c)], F32, tag="pp", name="pp", bufs=2)
+                nc.tensor.matmul_mx(
+                    out=pp[:],
+                    lhsT=cd[:, t * P:(t + 1) * P].bitcast(FP8X4), lhsT_scale=sc[:, t * P:(t + 1) * P],
+                    rhs=uc[:].bitcast(FP8X4), rhs_scale=us[:],
+                    start=True, stop=True,
+                )
+                pp_t[(g, ri)] = pp
+
+        def pe_xb(q):
+            c, j = divmod(q, 4)
+            if j >= mt(c):
+                return
+            for ri in range(2):
+                xn = psum.tile([P, 4, P], F32, tag="xn", name="xn", bufs=2)
+                for t in range(4):
+                    nc.tensor.transpose(xn[:, t, :], xT_t[c][ri][:, t, j * P:(j + 1) * P], ident[:])
+                xn_t[(q, ri)] = xn
+
+        def pe_m2(yi, spare_banks):
+            c, j = divmod(yi, 4)
+            if j >= mt(c):
+                return
+            tg = "pp" if (spare_banks and yi % 3 != 0) else "yy"
+            yy = psum.tile([P, WIDTH], F32, tag=tg, name="yy", bufs=(1 if tg == "yy" else 2))
+            for ri in range(2):
+                xc, xs = xq_t[(c, ri)]
+                cd, sc = c_cd[ri]
+                nc.tensor.matmul_mx(
+                    out=yy[:],
+                    lhsT=xc[:, j * P:(j + 1) * P].bitcast(FP8X4), lhsT_scale=xs[:, j * P:(j + 1) * P],
+                    rhs=cd[:].bitcast(FP8X4), rhs_scale=sc[:],
+                    start=(ri == 0), stop=(ri == 1),
+                )
+            yy_t[yi] = yy
+
+        def act_ut(c, hc):
+            if c not in gu_t:
+                gu_t[c] = work.tile([P, 4 * rows(c)], BF16, tag="gu", name="gu", align_bytes=64)
+            gu_w = gu_t[c][:].bitcast(F32).rearrange("p (m u) -> p m u", u=2)
+            nc.scalar.copy(out=gu_w[:, hc * 256:(hc + 1) * 256, :], in_=ut_t[(c, hc)][:].rearrange("p u m -> p m u"))
+
+        def act_a(g):
+            c, t = divmod(g, 4)
+            u, e = divmod(t, 2)
+            if t == 0:
+                xre = work.tile([P, 4, rows(c)], F32, tag="xTre", name="xTre", bufs=3)
+                xim = work.tile([P, 4, rows(c)], F32, tag="xTim", name="xTim", bufs=3)
+                xT_t[c] = (xre, xim)
+            xre, xim = xT_t[c]
+            s_re = st_t[(c, u, 0)]
+            nc.scalar.activation(out=xre[:, t, :], in_=s_re[:, :, e], func=ACTF.Copy, scale=lam_re[:, t:t + 1])
+            nc.scalar.activation(out=xim[:, t, :], in_=s_re[:, :, e], func=ACTF.Copy, scale=lam_im[:, t:t + 1])
+
+        def act_xn(q):
+            c, j = divmod(q, 4)
+            if j == 0:
+                xore = work.tile([P, mt(c), WIDTH], F32, tag="xore", name="xore")
+                xoim = work.tile([P, mt(c), WIDTH], F32, tag="xoim", name="xoim")
+                xo_t[c] = (xore, xoim)
+            if j >= mt(c):
+                return
+            for ri in range(2):
+                nc.scalar.copy(
+                    out=xo_t[c][ri][:, j, :].rearrange("p (q t) -> p q t", t=4),
+                    in_=xn_t[(q, ri)][:].rearrange("p t q -> p q t"),
+                )
+
+        def dve_b(g):
+            c, t = divmod(g, 4)
+            u, e = divmod(t, 2)
+            xre, xim = xT_t[c]
+            s_im = st_t[(c, u, 1)]
+            nc.vector.scalar_tensor_tensor(
+                out=xre[:, t, :], in0=s_im[:, :, e], scalar=nlam_im[:, t:t + 1], in1=xre[:, t, :],
+                op0=ALU.mult, op1=ALU.add,
+            )
+            nc.vector.scalar_tensor_tensor(
+                out=xim[:, t, :], in0=s_im[:, :, e], scalar=lam_re[:, t:t + 1], in1=xim[:, t, :],
+                op0=ALU.mult, op1=ALU.add,
+            )
+
+        def dve_x(g):
+            c, t = divmod(g, 4)
+            for ri in range(2):
+                x = xT_t[c][ri]
+                nc.vector.scalar_tensor_tensor(
+                    out=x[:, t, :], in0=pp_t[(g, ri)][:], scalar=gam[:, t:t + 1], in1=x[:, t, :],
+                    op0=ALU.mult, op1=ALU.add,
+                )
+
+        def dve_qu(c):
+            uc = work.tile([P, rows(c)], U32, tag="uc", name="uc", align_bytes=64)
+            us = work.tile([P, rows(c)], U8, tag="us", name="us", align_bytes=64)
+            nc.vector.quantize_mx(out=uc[:].bitcast(FP8X4), scales=us[:], in_=gu_t[c][:])
+            uq_t[c] = (uc, us)
+
+        def dve_qx(c, ri):
+            tg = ("re", "im")[ri]
+            xc = work.tile([P, rows(c)], U32, tag="xc" + tg, name="xc" + tg, align_bytes=64)
+            xs = work.tile([P, rows(c)], U8, tag="xs" + tg, name="xs" + tg, align_bytes=64)
+            nc.vector.quantize_mx(out=xc[:].bitcast(FP8X4), scales=xs[:], in_=gx_t[(c, ri)][:])
+            xq_t[(c, ri)] = (xc, xs)
+
+        def dve_y(yi):
+            c, j = divmod(yi, 4)
+            if j >= mt(c):
+                return
+            if j == 0:
+                yo_t[c] = work.tile([P, mt(c), WIDTH], F32, tag="yo", name="yo")
+            if mt(c) == 4 and j == Y_OFF:
+                nc.scalar.copy(out=yo_t[c][:, j, :], in_=yy_t[yi][:])
+                nc.gpsimd.tensor_tensor(out=yo_t[c][:, j, :], in0=yo_t[c][:, j, :], in1=du_t[c][:, j, :], op=ALU.add)
+            else:
+                nc.vector.tensor_tensor(out=yo_t[c][:, j, :], in0=yy_t[yi][:], in1=du_t[c][:, j, :], op=ALU.add)
+            if j == mt(c) - 1:
+                store(out_0, c, yo_t[c])
+
+        def pool_du(c):
+            du = work.tile([P, mt(c), WIDTH], F32, tag="du", name="du", align_bytes=64)
+            nc.gpsimd.tensor_tensor(
+                out=du[:],
+                in0=u_t[c][:].rearrange("p (j k) -> p j k", j=mt(c)),
+                in1=dbc[:].unsqueeze(1).to_broadcast([P, mt(c), WIDTH]),
+                op=ALU.mult,
+            )
+            du_t[c] = du
+
+        def cast_x(c, ri, engs):
+            tg = ("gxre", "gxim")[ri]
+            gx = work.tile([P, 4 * rows(c)], BF16, tag=tg, name=tg, align_bytes=64)
+            part = rows(c) // len(engs)
+            for i, eng in enumerate(engs):
+                dst = gx[:, 4 * part * i:4 * part * (i + 1)].rearrange("p (m t) -> p m t", t=4)
+                src = xT_t[c][ri][:, :, part * i:part * (i + 1)].rearrange("p t m -> p m t")
+                if eng == "a":
+                    nc.scalar.copy(out=dst, in_=src)
+                else:
+                    nc.gpsimd.tensor_scalar(out=dst, in0=src, scalar1=1.0, scalar2=0.0, op0=ALU.mult, op1=ALU.add)
+            gx_t[(c, ri)] = gx
+
+        def store(dram, c, src):
+            nc.sync.dma_start(out=rows_of(dram, c).rearrange("(i j) h -> i j h", j=mt(c)), in_=src[:])
+
+        def ut_at(g):
+            c, k = divmod(g, 4)
+            w = None
+            if g in (-7, -5):
+                w = (0, (g + 7) // 2)
+            elif g in (0, 1):
+                w = (1, g)
+            elif c >= 0 and k >= 2 and ok(c + 2):
+                w = (c + 2, k - 2)
+            if w is not None and 2 * w[1] >= mt(w[0]):
+                w = None
+            return w
+
+        for g in range(-8, NPL + YLAG):
+            c, k = divmod(g, 4)
+            if okp(g):
+                dve_x(g)
+            if g == -4:
+                dve_qu(0)
+            if k == KQ:
+                if ok(c - 1):
+                    dve_qx(c - 1, 0)
+                    dve_qx(c - 1, 1)
+                if c == 1:
+                    c_cd.append(quant(g_c[:, 0, :], "cre"))
+                    c_cd.append(quant(g_c[:, 1, :], "cim"))
+                if c >= 0 and ok(c + 1):
+                    dve_qu(c + 1)
+            if okp(g - YLAG):
+                dve_y(g - YLAG)
+            if okp(g + 2):
+                act_a(g + 2)
+            if k == KQ and ok(c):
+                pool_du(c)
+            if k == 3 and ok(c):
+                cast_x(c, 0, "g")
+                cast_x(c, 1, "a" if c == NCH - 1 else "ga")
+            if okp(g - 4):
+                act_xn(g - 4)
+            if ut_at(g) is not None:
+                act_ut(ut_at(g)[0], ut_at(g)[1])
+            if k == 2 and c >= 0:
+                if ok(c + 3):
+                    load_s(c + 3)
+                if ok(c + 4):
+                    load_u(c + 4)
+            if k == 3 and ok(c - 1):
+                store(out_1, c - 1, xo_t[c - 1][0])
+                store(out_2, c - 1, xo_t[c - 1][1])
+            if okp(g + 1) and (g + 1) % 2 == 0:
+                pe_st((g + 1) // 4, ((g + 1) % 4) // 2, 1)
+            if okp(g + 1):
+                pe_m1(g + 1)
+            if okp(g + 1 - YLAG):
+                pe_m2(g + 1 - YLAG, g >= NPL - 1)
+            if ut_at(g + 1) is not None:
+                pe_ut(ut_at(g + 1)[0], ut_at(g + 1)[1])
+            if okp(g + 3) and (g + 3) % 2 == 0:
+                pe_st((g + 3) // 4, ((g + 3) % 4) // 2, 0)
+            if okp(g - 3):
+                pe_xb(g - 3)
+            if okp(g + 1):
+                dve_b(g + 1)

@@ -106,6 +106,8 @@ def tile_linearrecurrentunitcell_t_kernel(
 
         ident = const.tile([P, P], F32, name="ident")
         make_identity(nc, ident[:])
+        ident_b = const.tile([P, P], BF16, name="ident_b")
+        make_identity(nc, ident_b[:])
 
         def small(nm, dt=F32):
             return const.tile([P, 4], dt, name=nm)
@@ -204,13 +206,24 @@ def tile_linearrecurrentunitcell_t_kernel(
                     )
             ut_t[(c, hc)] = ut
 
-        def pe_st(c, u, which):
-            src_t, tg = ((sre_t, "str"), (sim_t, "sti"))[which]
-            s_w = src_t[c][:].bitcast(F32)
-            st = psum.tile([P, rows(c)], F32, tag=tg, name=tg)
+        def pe_sti(c, u):
+            s_w = sim_t[c][:].bitcast(F32)
+            st = psum.tile([P, rows(c)], F32, tag="sti", name="sti")
             for j in range(mt(c)):
                 nc.tensor.transpose(st[:, j * P:(j + 1) * P], s_w[:, j * 256 + u:(j + 1) * 256:2], ident[:])
-            st_t[(c, u, which)] = st[:].bitcast(BF16).rearrange("p (m e) -> p m e", e=2)
+            st_t[(c, u, 1)] = st[:].bitcast(BF16).rearrange("p (m e) -> p e m", e=2)
+
+        def pe_str(c, u):
+            s_b = sre_t[c]
+            st = psum.tile([P, 2, rows(c)], BF16, tag="str", name="str")
+            for e in range(2):
+                t = 2 * u + e
+                for j in range(mt(c)):
+                    nc.tensor.matmul(
+                        st[:, e, j * P:(j + 1) * P], lhsT=s_b[:, j * WIDTH + t:(j + 1) * WIDTH:4], rhs=ident_b[:],
+                        start=True, stop=True,
+                    )
+            st_t[(c, u, 0)] = st[:]
 
         def pe_m1(g):
             c, t = divmod(g, 4)
@@ -268,8 +281,8 @@ def tile_linearrecurrentunitcell_t_kernel(
                 xT_t[c] = (xre, xim)
             xre, xim = xT_t[c]
             s_re = st_t[(c, u, 0)]
-            nc.scalar.activation(out=xre[:, t, :], in_=s_re[:, :, e], func=ACTF.Copy, scale=lam_re[:, t:t + 1])
-            nc.scalar.activation(out=xim[:, t, :], in_=s_re[:, :, e], func=ACTF.Copy, scale=lam_im[:, t:t + 1])
+            nc.scalar.activation(out=xre[:, t, :], in_=s_re[:, e, :], func=ACTF.Copy, scale=lam_re[:, t:t + 1])
+            nc.scalar.activation(out=xim[:, t, :], in_=s_re[:, e, :], func=ACTF.Copy, scale=lam_im[:, t:t + 1])
 
         def act_xn(q):
             c, j = divmod(q, 4)
@@ -291,11 +304,11 @@ def tile_linearrecurrentunitcell_t_kernel(
             xre, xim = xT_t[c]
             s_im = st_t[(c, u, 1)]
             nc.vector.scalar_tensor_tensor(
-                out=xre[:, t, :], in0=s_im[:, :, e], scalar=nlam_im[:, t:t + 1], in1=xre[:, t, :],
+                out=xre[:, t, :], in0=s_im[:, e, :], scalar=nlam_im[:, t:t + 1], in1=xre[:, t, :],
                 op0=ALU.mult, op1=ALU.add,
             )
             nc.vector.scalar_tensor_tensor(
-                out=xim[:, t, :], in0=s_im[:, :, e], scalar=lam_re[:, t:t + 1], in1=xim[:, t, :],
+                out=xim[:, t, :], in0=s_im[:, e, :], scalar=lam_re[:, t:t + 1], in1=xim[:, t, :],
                 op0=ALU.mult, op1=ALU.add,
             )
 
@@ -411,15 +424,15 @@ def tile_linearrecurrentunitcell_t_kernel(
                 store(out_1, c - 1, xo_t[c - 1][0])
                 store(out_2, c - 1, xo_t[c - 1][1])
             if okp(g + 1) and (g + 1) % 2 == 0:
-                pe_st((g + 1) // 4, ((g + 1) % 4) // 2, 1)
+                pe_sti((g + 1) // 4, ((g + 1) % 4) // 2)
             if okp(g + 1):
                 pe_m1(g + 1)
             if okp(g + 1 - YLAG):
                 pe_m2(g + 1 - YLAG, g >= NPL - 1)
+            if okp(g + 3) and (g + 3) % 2 == 0:
+                pe_str((g + 3) // 4, ((g + 3) % 4) // 2)
             if ut_at(g + 1) is not None:
                 pe_ut(ut_at(g + 1)[0], ut_at(g + 1)[1])
-            if okp(g + 3) and (g + 3) % 2 == 0:
-                pe_st((g + 3) // 4, ((g + 3) % 4) // 2, 0)
             if okp(g - 3):
                 pe_xb(g - 3)
             if okp(g + 1):

@@ -54,16 +54,20 @@ def tile_linearrecurrentunitcell_t_kernel(
         def mt(c):
             return CHUNKS[c] // P
 
-        pr_nu = const.tile([P, 4], BF16, name="pr_nu")
         pr_th = const.tile([P, 4], BF16, name="pr_th")
+        pr_nu = const.tile([P, 4], BF16, name="pr_nu")
         pr_ga = const.tile([P, 4], BF16, name="pr_ga")
         with nc.allow_non_contiguous_dma(reason="three vectors of 512 values, four neighbours a piece"):
-            for dst, vec in ((pr_nu, nu), (pr_th, theta), (pr_ga, gamma)):
+            for dst, vec in ((pr_th, theta), (pr_nu, nu), (pr_ga, gamma)):
                 nc.scalar.dma_start(
                     out=dst[:], in_=vec.rearrange("(p t) -> p t", t=4),
                 )
         dbc = const.tile([P, WIDTH], BF16, name="dbc")
         nc.scalar.dma_start(out=dbc[:], in_=D.partition_broadcast(P))
+        warm = const.tile([P, 1], F32, name="warm")
+        nc.vector.memset(warm[:], 0.0)
+        warm_out = const.tile([P, 1], F32, name="warm_out")
+        nc.scalar.activation(out=warm_out[:], in_=warm[:], func=ACTF.Exp)
 
         u_t = {}
         sre_t = {}
@@ -93,13 +97,13 @@ def tile_linearrecurrentunitcell_t_kernel(
             return raw
 
         raw_bre = load_w(B_re, "bre", "xore")
-        raw_bim = load_w(B_im, "bim", "xore")
         load_u(0)
+        raw_bim = load_w(B_im, "bim", "xore")
         load_s(0)
         load_u(1)
+        load_s(1)
         raw_cre = load_w(C_re, "cre", "xoim")
         raw_cim = load_w(C_im, "cim", "xoim")
-        load_s(1)
         load_u(2)
         load_s(2)
         load_u(3)
@@ -118,28 +122,21 @@ def tile_linearrecurrentunitcell_t_kernel(
             nc.vector.quantize_mx(out=cd[:].bitcast(FP8X4), scales=sc[:], in_=g_ap)
             return cd, sc
 
-        def regroup_b(raw, nm):
-            g = work.tile([P, 4 * WIDTH], BF16, tag="gxre", name="g_" + nm, align_bytes=64)
+        def regroup_b(raw, g, half):
             src = raw[:].rearrange("p (t q s) -> p s q t", t=4, s=4)
             dst = g[:].rearrange("p (s q t) -> p s q t", s=4, t=4)
-            for half in range(2):
-                nc.vector.tensor_copy(out=dst[:, 2 * half:2 * half + 2], in_=src[:, 2 * half:2 * half + 2])
-            return g
+            nc.vector.tensor_copy(out=dst[:, 2 * half:2 * half + 2], in_=src[:, 2 * half:2 * half + 2])
 
-        thf = small("thf")
-        nc.vector.tensor_copy(out=thf[:], in_=pr_th[:])
-        kq = small("kq")
-        nc.vector.tensor_scalar_mul(out=kq[:], in0=thf[:], scalar1=1.0 / (2.0 * math.pi))
         ki = small("ki", I32)
-        nc.vector.tensor_copy(out=ki[:], in_=kq[:])
-        kf = small("kf")
-        nc.vector.tensor_copy(out=kf[:], in_=ki[:])
+        nc.vector.tensor_scalar_mul(out=ki[:], in0=pr_th[:], scalar1=1.0 / (2.0 * math.pi))
+        g_bre = work.tile([P, 4 * WIDTH], BF16, tag="gxre", name="g_bre", align_bytes=64)
+        g_bim = work.tile([P, 4 * WIDTH], BF16, tag="gxre", name="g_bim", align_bytes=64)
+        regroup_b(raw_bre, g_bre, 0)
         r1 = small("r1")
-        nc.vector.scalar_tensor_tensor(out=r1[:], in0=kf[:], scalar=-TWO_PI_HI, in1=thf[:], op0=ALU.mult, op1=ALU.add)
+        nc.vector.scalar_tensor_tensor(out=r1[:], in0=ki[:], scalar=-TWO_PI_HI, in1=pr_th[:], op0=ALU.mult, op1=ALU.add)
+        regroup_b(raw_bre, g_bre, 1)
         r2 = small("r2")
-        nc.vector.scalar_tensor_tensor(out=r2[:], in0=kf[:], scalar=-TWO_PI_LO, in1=r1[:], op0=ALU.mult, op1=ALU.add)
-        gam = small("gam")
-        nc.vector.tensor_copy(out=gam[:], in_=pr_ga[:])
+        nc.vector.scalar_tensor_tensor(out=r2[:], in0=ki[:], scalar=-TWO_PI_LO, in1=r1[:], op0=ALU.mult, op1=ALU.add)
         e1 = small("e1")
         nc.scalar.activation(out=e1[:], in_=pr_nu[:], func=ACTF.Exp)
         mag = small("mag")
@@ -148,28 +145,24 @@ def tile_linearrecurrentunitcell_t_kernel(
         nc.scalar.activation(out=sa[:], in_=r2[:], func=ACTF.Sin, scale=0.5)
         sb = small("sb")
         nc.scalar.activation(out=sb[:], in_=r2[:], func=ACTF.Sin, scale=0.25)
-
-        g_bre = regroup_b(raw_bre, "bre")
-        g_bim = regroup_b(raw_bim, "bim")
-
-        sa2 = small("sa2")
-        nc.vector.tensor_tensor(out=sa2[:], in0=sa[:], in1=sa[:], op=ALU.mult)
-        cosr = small("cosr")
-        nc.vector.tensor_scalar(out=cosr[:], in0=sa2[:], scalar1=-2.0, scalar2=1.0, op0=ALU.mult, op1=ALU.add)
+        regroup_b(raw_bim, g_bim, 0)
+        regroup_b(raw_bim, g_bim, 1)
+        b_cd = [quant(g_bre[:], "bre")]
+        sam = small("sam")
+        nc.vector.tensor_tensor(out=sam[:], in0=sa[:], in1=mag[:], op=ALU.mult)
         sb2 = small("sb2")
         nc.vector.tensor_tensor(out=sb2[:], in0=sb[:], in1=sb[:], op=ALU.mult)
+        b_cd.append(quant(g_bim[:], "bim"))
+        ss = small("ss")
+        nc.vector.tensor_tensor(out=ss[:], in0=sa[:], in1=sam[:], op=ALU.mult)
         ch2 = small("ch2")
         nc.vector.tensor_scalar(out=ch2[:], in0=sb2[:], scalar1=-4.0, scalar2=2.0, op0=ALU.mult, op1=ALU.add)
-        sinr = small("sinr")
-        nc.vector.tensor_tensor(out=sinr[:], in0=sa[:], in1=ch2[:], op=ALU.mult)
         lam_re = small("lam_re")
-        nc.vector.tensor_tensor(out=lam_re[:], in0=mag[:], in1=cosr[:], op=ALU.mult)
+        nc.vector.scalar_tensor_tensor(out=lam_re[:], in0=ss[:], scalar=-2.0, in1=mag[:], op0=ALU.mult, op1=ALU.add)
         lam_im = small("lam_im")
-        nc.vector.tensor_tensor(out=lam_im[:], in0=mag[:], in1=sinr[:], op=ALU.mult)
+        nc.vector.tensor_tensor(out=lam_im[:], in0=sam[:], in1=ch2[:], op=ALU.mult)
         nlam_im = small("nlam_im")
-        nc.vector.tensor_scalar_mul(out=nlam_im[:], in0=lam_im[:], scalar1=-1.0)
-
-        b_cd = [quant(g_bre[:], "bre"), quant(g_bim[:], "bim")]
+        nc.vector.scalar_tensor_tensor(out=nlam_im[:], in0=sam[:], scalar=-1.0, in1=ch2[:], op0=ALU.mult, op1=ALU.mult)
         c_cd = []
 
         gu_t = {}
@@ -317,7 +310,7 @@ def tile_linearrecurrentunitcell_t_kernel(
             for ri in range(2):
                 x = xT_t[c][ri]
                 nc.vector.scalar_tensor_tensor(
-                    out=x[:, t, :], in0=pp_t[(g, ri)][:], scalar=gam[:, t:t + 1], in1=x[:, t, :],
+                    out=x[:, t, :], in0=pp_t[(g, ri)][:], scalar=pr_ga[:, t:t + 1], in1=x[:, t, :],
                     op0=ALU.mult, op1=ALU.add,
                 )
 
@@ -339,7 +332,7 @@ def tile_linearrecurrentunitcell_t_kernel(
             if j >= mt(c):
                 return
             if j == 0:
-                yo_t[c] = work.tile([P, mt(c), WIDTH], F32, tag="yo", name="yo")
+                yo_t[c] = work.tile([P, mt(c), WIDTH], F32, tag="yo", name="yo", bufs=3)
             if mt(c) == 4 and j == Y_OFF:
                 nc.scalar.copy(out=yo_t[c][:, j, :], in_=yy_t[yi][:])
                 nc.gpsimd.tensor_tensor(out=yo_t[c][:, j, :], in0=yo_t[c][:, j, :], in1=du_t[c][:, j, :], op=ALU.add)
@@ -367,6 +360,8 @@ def tile_linearrecurrentunitcell_t_kernel(
                 src = xT_t[c][ri][:, :, part * i:part * (i + 1)].rearrange("p t m -> p m t")
                 if eng == "a":
                     nc.scalar.copy(out=dst, in_=src)
+                elif eng == "v":
+                    nc.vector.tensor_copy(out=dst, in_=src)
                 else:
                     nc.gpsimd.tensor_scalar(out=dst, in0=src, scalar1=1.0, scalar2=0.0, op0=ALU.mult, op1=ALU.add)
             gx_t[(c, ri)] = gx
@@ -409,7 +404,7 @@ def tile_linearrecurrentunitcell_t_kernel(
             if k == KQ and ok(c):
                 pool_du(c)
             if k == 3 and ok(c):
-                cast_x(c, 0, "g")
+                cast_x(c, 0, "v" if c == NCH - 1 else "g")
                 cast_x(c, 1, "a" if c == NCH - 1 else "ga")
             if okp(g - 4):
                 act_xn(g - 4)

@@ -179,7 +179,6 @@ def tile_linearrecurrentunitcell_t_kernel(
         xn_t = {}
         yy_t = {}
 
-        gu_t[1] = work.tile([P, 4 * rows(1)], BF16, tag="du", name="gu1", align_bytes=64)
         g_c = work.tile([P, 2, 4 * WIDTH], BF16, tag="du", name="g_c", align_bytes=64)
         for ri, (raw, sign) in enumerate(((raw_cre, 1.0), (raw_cim, -1.0))):
             nc.gpsimd.tensor_scalar(
@@ -341,6 +340,10 @@ def tile_linearrecurrentunitcell_t_kernel(
             if j == mt(c) - 1:
                 store(out_0, c, yo_t[c])
 
+        def pool_behind(codes):
+            tok = work.tile([P, 1], U32, tag="tok", name="tok")
+            nc.gpsimd.tensor_copy(out=tok[:], in_=codes[:, 0:1])
+
         def pool_du(c):
             du = work.tile([P, mt(c), WIDTH], F32, tag="du", name="du", align_bytes=64)
             nc.gpsimd.tensor_tensor(
@@ -386,30 +389,34 @@ def tile_linearrecurrentunitcell_t_kernel(
             c, k = divmod(g, 4)
             if okp(g):
                 dve_x(g)
+            if okp(g - YLAG):
+                dve_y(g - YLAG)
             if g == -4:
                 dve_qu(0)
             if k == KQ:
-                if ok(c - 1):
-                    dve_qx(c - 1, 0)
-                    dve_qx(c - 1, 1)
+                quantised = None
+                if c >= 0 and ok(c + 1):
+                    dve_qu(c + 1)
+                    quantised = uq_t[c + 1][0]
                 if c == 1:
                     c_cd.append(quant(g_c[:, 0, :], "cre"))
                     c_cd.append(quant(g_c[:, 1, :], "cim"))
-                if c >= 0 and ok(c + 1):
-                    dve_qu(c + 1)
-            if okp(g - YLAG):
-                dve_y(g - YLAG)
-            if okp(g + 2):
-                act_a(g + 2)
-            if k == KQ and ok(c):
-                pool_du(c)
-            if k == 3 and ok(c):
-                cast_x(c, 0, "v" if c == NCH - 1 else "g")
-                cast_x(c, 1, "a" if c == NCH - 1 else "ga")
+                if ok(c - 1):
+                    dve_qx(c - 1, 0)
+                    dve_qx(c - 1, 1)
+                    quantised = xq_t[(c - 1, 1)][0]
+                if ok(c):
+                    pool_behind(quantised)
+                    pool_du(c)
             if okp(g - 4):
                 act_xn(g - 4)
             if ut_at(g) is not None:
                 act_ut(ut_at(g)[0], ut_at(g)[1])
+            if okp(g + 2):
+                act_a(g + 2)
+            if k == 3 and ok(c):
+                cast_x(c, 0, "v" if c == NCH - 1 else "g")
+                cast_x(c, 1, "a" if c == NCH - 1 else "ga")
             if k == 2 and c >= 0:
                 if ok(c + 3):
                     load_s(c + 3)
@@ -424,11 +431,11 @@ def tile_linearrecurrentunitcell_t_kernel(
                 pe_m1(g + 1)
             if okp(g + 1 - YLAG):
                 pe_m2(g + 1 - YLAG, g >= NPL - 1)
+            if okp(g - 3):
+                pe_xb(g - 3)
             if okp(g + 3) and (g + 3) % 2 == 0:
                 pe_str((g + 3) // 4, ((g + 3) % 4) // 2)
             if ut_at(g + 1) is not None:
                 pe_ut(ut_at(g + 1)[0], ut_at(g + 1)[1])
-            if okp(g - 3):
-                pe_xb(g - 3)
             if okp(g + 1):
                 dve_b(g + 1)

@@ -62,8 +62,6 @@ def tile_linearrecurrentunitcell_t_kernel(
                 nc.scalar.dma_start(
                     out=dst[:], in_=vec.rearrange("(p t) -> p t", t=4),
                 )
-        dbc = const.tile([P, WIDTH], BF16, name="dbc")
-        nc.scalar.dma_start(out=dbc[:], in_=D.partition_broadcast(P))
         warm = const.tile([P, 1], F32, name="warm")
         nc.vector.memset(warm[:], 0.0)
         warm_out = const.tile([P, 1], F32, name="warm_out")
@@ -102,6 +100,8 @@ def tile_linearrecurrentunitcell_t_kernel(
         load_s(0)
         load_u(1)
         load_s(1)
+        dbc = const.tile([P, WIDTH], BF16, name="dbc")
+        nc.sync.dma_start(out=dbc[:], in_=D.partition_broadcast(P))
         raw_cre = load_w(C_re, "cre", "xoim")
         raw_cim = load_w(C_im, "cim", "xoim")
         load_u(2)

@@ -2,7 +2,6 @@ from contextlib import ExitStack
 import math
 
 import concourse.mybir as mybir
-from concourse.masks import make_identity
 
 F32 = mybir.dt.float32
 BF16 = mybir.dt.bfloat16
@@ -108,10 +107,22 @@ def tile_linearrecurrentunitcell_t_kernel(
         load_s(2)
         load_u(3)
 
+        ones = const.tile([P, P], F32, name="ones")
+        nc.vector.memset(ones[:], 1.0)
+        col_no = const.tile([P, P], F32, name="col_no")
+        nc.vector.tensor_tensor_scan(
+            out=col_no[:], data0=ones[:], data1=ones[:], initial=0.0, op0=ALU.mult, op1=ALU.add
+        )
+        col_no_b = const.tile([P, P], BF16, name="col_no_b")
+        nc.vector.tensor_copy(out=col_no_b[:], in_=col_no[:])
+        share = const.tile([P, P], BF16, name="share")
+        nc.vector.memset(share[:], 1.0 / P)
+        row_no = psum.tile([P, P], F32, tag="yy", name="row_no")
+        nc.tensor.matmul(row_no[:], lhsT=col_no_b[:], rhs=share[:], start=True, stop=True)
         ident = const.tile([P, P], F32, name="ident")
-        make_identity(nc, ident[:])
+        nc.vector.tensor_tensor(out=ident[:], in0=row_no[:], in1=col_no[:], op=ALU.is_equal)
         ident_b = const.tile([P, P], BF16, name="ident_b")
-        make_identity(nc, ident_b[:])
+        nc.vector.tensor_copy(out=ident_b[:], in_=ident[:])
 
         def small(nm, dt=F32):
             return const.tile([P, 4], dt, name=nm)

@@ -159,6 +159,8 @@ def tile_linearrecurrentunitcell_t_kernel(
         regroup_b(raw_bim, g_bim, 0)
         regroup_b(raw_bim, g_bim, 1)
         b_cd = [quant(g_bre[:], "bre")]
+        gam = small("gam")
+        nc.vector.tensor_copy(out=gam[:], in_=pr_ga[:])
         sam = small("sam")
         nc.vector.tensor_tensor(out=sam[:], in0=sa[:], in1=mag[:], op=ALU.mult)
         sb2 = small("sb2")
@@ -190,7 +192,7 @@ def tile_linearrecurrentunitcell_t_kernel(
         xn_t = {}
         yy_t = {}
 
-        g_c = work.tile([P, 2, 4 * WIDTH], BF16, tag="du", name="g_c", align_bytes=64)
+        g_c = work.tile([P, 2, 4 * WIDTH], BF16, tag="du", name="g_c", bufs=3, align_bytes=64)
         for ri, (raw, sign) in enumerate(((raw_cre, 1.0), (raw_cim, -1.0))):
             nc.gpsimd.tensor_scalar(
                 out=g_c[:, ri, :].rearrange("p (n t) -> p n t", t=4),
@@ -320,7 +322,7 @@ def tile_linearrecurrentunitcell_t_kernel(
             for ri in range(2):
                 x = xT_t[c][ri]
                 nc.vector.scalar_tensor_tensor(
-                    out=x[:, t, :], in0=pp_t[(g, ri)][:], scalar=pr_ga[:, t:t + 1], in1=x[:, t, :],
+                    out=x[:, t, :], in0=pp_t[(g, ri)][:], scalar=gam[:, t:t + 1], in1=x[:, t, :],
                     op0=ALU.mult, op1=ALU.add,
                 )
 
@@ -348,15 +350,18 @@ def tile_linearrecurrentunitcell_t_kernel(
                 nc.gpsimd.tensor_tensor(out=yo_t[c][:, j, :], in0=yo_t[c][:, j, :], in1=du_t[c][:, j, :], op=ALU.add)
             else:
                 nc.vector.tensor_tensor(out=yo_t[c][:, j, :], in0=yy_t[yi][:], in1=du_t[c][:, j, :], op=ALU.add)
-            if j == mt(c) - 1:
-                store(out_0, c, yo_t[c])
+            if j % 2 == 1:
+                pair = slice(j - 1, j + 1)
+                nc.sync.dma_start(
+                    out=rows_of(out_0, c).rearrange("(i j) h -> i j h", j=mt(c))[:, pair, :], in_=yo_t[c][:, pair, :]
+                )
 
         def pool_behind(codes):
             tok = work.tile([P, 1], U32, tag="tok", name="tok")
             nc.gpsimd.tensor_copy(out=tok[:], in_=codes[:, 0:1])
 
         def pool_du(c):
-            du = work.tile([P, mt(c), WIDTH], F32, tag="du", name="du", align_bytes=64)
+            du = work.tile([P, mt(c), WIDTH], F32, tag="du", name="du", bufs=3, align_bytes=64)
             nc.gpsimd.tensor_tensor(
                 out=du[:],
                 in0=u_t[c][:].rearrange("p (j k) -> p j k", j=mt(c)),
@@ -412,13 +417,16 @@ def tile_linearrecurrentunitcell_t_kernel(
                 if c == 1:
                     c_cd.append(quant(g_c[:, 0, :], "cre"))
                     c_cd.append(quant(g_c[:, 1, :], "cim"))
-                if ok(c - 1):
+                if ok(c - 1) and c - 1 != NCH - 1:
                     dve_qx(c - 1, 0)
                     dve_qx(c - 1, 1)
                     quantised = xq_t[(c - 1, 1)][0]
-                if ok(c):
+                if ok(c) and c != NCH - 1:
                     pool_behind(quantised)
                     pool_du(c)
+            if g == NPL:
+                dve_qx(NCH - 1, 0)
+                dve_qx(NCH - 1, 1)
             if okp(g - 4):
                 act_xn(g - 4)
             if ut_at(g) is not None:
@@ -427,7 +435,9 @@ def tile_linearrecurrentunitcell_t_kernel(
                 act_a(g + 2)
             if k == 3 and ok(c):
                 cast_x(c, 0, "v" if c == NCH - 1 else "g")
-                cast_x(c, 1, "a" if c == NCH - 1 else "ga")
+                cast_x(c, 1, "va" if c == NCH - 1 else "ga")
+                if c == NCH - 2:
+                    pool_du(NCH - 1)
             if k == 2 and c >= 0:
                 if ok(c + 3):
                     load_s(c + 3)

from contextlib import ExitStack
import math

import concourse.mybir as mybir

F32 = mybir.dt.float32
BF16 = mybir.dt.bfloat16
U32 = mybir.dt.uint32
U8 = mybir.dt.uint8
I32 = mybir.dt.int32
FP8X4 = mybir.dt.float8_e4m3fn_x4
ALU = mybir.AluOpType
ACTF = mybir.ActivationFunctionType

P = 128
ROWS = 4096
WIDTH = 512
FLOPS = 4 * 2 * ROWS * WIDTH * WIDTH

TWO_PI_HI = 6.28125
TWO_PI_LO = 2.0 * math.pi - 6.28125
CHUNKS = [512] * 7 + [256, 256]

NCH = len(CHUNKS)
NPL = 4 * NCH
OFFS = [sum(CHUNKS[:c]) for c in range(NCH)]
assert sum(CHUNKS) == ROWS
YLAG = 7
Y_OFF = -1
KQ = 2


def tile_linearrecurrentunitcell_t_kernel(
    tc, inputs, state_re, state_im, B_re, B_im, C_re, C_im, D, nu, theta, gamma, out_0, out_1, out_2
):
    nc = tc.nc
    with ExitStack() as ctx:
        ctx.enter_context(tc.manual_schedule())
        const = ctx.enter_context(tc.tile_pool(name="const", bufs=1))
        io = ctx.enter_context(tc.tile_pool(name="io", bufs=3))
        work = ctx.enter_context(tc.tile_pool(name="work", bufs=2))
        psum = ctx.enter_context(tc.psum_pool(name="psum", bufs=1))

        def ok(c):
            return 0 <= c < NCH

        def okp(g):
            return 0 <= g < NPL

        def rows(c):
            return CHUNKS[c]

        def mt(c):
            return CHUNKS[c] // P

        pr_th = const.tile([P, 4], BF16, name="pr_th")
        pr_nu = const.tile([P, 4], BF16, name="pr_nu")
        pr_ga = const.tile([P, 4], BF16, name="pr_ga")
        with nc.allow_non_contiguous_dma(reason="three vectors of 512 values, four neighbours a piece"):
            for dst, vec in ((pr_th, theta), (pr_nu, nu), (pr_ga, gamma)):
                nc.scalar.dma_start(
                    out=dst[:], in_=vec.rearrange("(p t) -> p t", t=4),
                )
        warm = const.tile([P, 1], F32, name="warm")
        nc.vector.memset(warm[:], 0.0)
        warm_out = const.tile([P, 1], F32, name="warm_out")
        nc.scalar.activation(out=warm_out[:], in_=warm[:], func=ACTF.Exp)

        u_t = {}
        sre_t = {}
        sim_t = {}

        def rows_of(dram, c):
            return dram[OFFS[c]:OFFS[c] + rows(c), :]

        def load_u(c):
            u_sb = io.tile([P, mt(c) * WIDTH], BF16, tag="u", name="u_sb", bufs=4)
            nc.sync.dma_start(out=u_sb[:], in_=rows_of(inputs, c).rearrange("(i j) k -> i (j k)", j=mt(c)))
            u_t[c] = u_sb

        def load_s(c):
            sre = io.tile([P, mt(c) * WIDTH], BF16, tag="sre", name="sre")
            nc.sync.dma_start(out=sre[:], in_=rows_of(state_re, c).rearrange("(i j) k -> i (j k)", j=mt(c)))
            sre_t[c] = sre
            sim = io.tile([P, mt(c) * WIDTH], BF16, tag="sim", name="sim")
            nc.sync.dma_start(out=sim[:], in_=rows_of(state_im, c).rearrange("(i j) k -> i (j k)", j=mt(c)))
            sim_t[c] = sim

        def load_w(w, nm, tg):
            raw = work.tile([P, 4 * WIDTH], BF16, tag=tg, name="raw_" + nm)
            nc.sync.dma_start(
                out=raw[:], in_=w.rearrange("(p t) c -> p (t c)", t=4),
            )
            return raw

        raw_bre = load_w(B_re, "bre", "xore")
        load_u(0)
        raw_bim = load_w(B_im, "bim", "xore")
        load_s(0)
        load_u(1)
        load_s(1)
        dbc = const.tile([P, WIDTH], BF16, name="dbc")
        nc.sync.dma_start(out=dbc[:], in_=D.partition_broadcast(P))
        raw_cre = load_w(C_re, "cre", "xoim")
        raw_cim = load_w(C_im, "cim", "xoim")
        load_u(2)
        load_s(2)
        load_u(3)

        ones = const.tile([P, P], F32, name="ones")
        nc.vector.memset(ones[:], 1.0)
        col_no = const.tile([P, P], F32, name="col_no")
        nc.vector.tensor_tensor_scan(
            out=col_no[:], data0=ones[:], data1=ones[:], initial=0.0, op0=ALU.mult, op1=ALU.add
        )
        col_no_b = const.tile([P, P], BF16, name="col_no_b")
        nc.vector.tensor_copy(out=col_no_b[:], in_=col_no[:])
        share = const.tile([P, P], BF16, name="share")
        nc.vector.memset(share[:], 1.0 / P)
        row_no = psum.tile([P, P], F32, tag="yy", name="row_no")
        nc.tensor.matmul(row_no[:], lhsT=col_no_b[:], rhs=share[:], start=True, stop=True)
        ident = const.tile([P, P], F32, name="ident")
        nc.vector.tensor_tensor(out=ident[:], in0=row_no[:], in1=col_no[:], op=ALU.is_equal)
        ident_b = const.tile([P, P], BF16, name="ident_b")
        nc.vector.tensor_copy(out=ident_b[:], in_=ident[:])

        def small(nm, dt=F32):
            return const.tile([P, 4], dt, name=nm)

        def quant(g_ap, nm):
            cd = const.tile([P, WIDTH], U32, name="cd_" + nm, align_bytes=64)
            sc = const.tile([P, WIDTH], U8, name="sc_" + nm, align_bytes=64)
            nc.vector.quantize_mx(out=cd[:].bitcast(FP8X4), scales=sc[:], in_=g_ap)
            return cd, sc

        def regroup_b(raw, g, half):
            src = raw[:].rearrange("p (t q s) -> p s q t", t=4, s=4)
            dst = g[:].rearrange("p (s q t) -> p s q t", s=4, t=4)
            nc.vector.tensor_copy(out=dst[:, 2 * half:2 * half + 2], in_=src[:, 2 * half:2 * half + 2])

        ki = small("ki", I32)
        nc.vector.tensor_scalar_mul(out=ki[:], in0=pr_th[:], scalar1=1.0 / (2.0 * math.pi))
        g_bre = work.tile([P, 4 * WIDTH], BF16, tag="gxre", name="g_bre", align_bytes=64)
        g_bim = work.tile([P, 4 * WIDTH], BF16, tag="gxre", name="g_bim", align_bytes=64)
        regroup_b(raw_bre, g_bre, 0)
        r1 = small("r1")
        nc.vector.scalar_tensor_tensor(out=r1[:], in0=ki[:], scalar=-TWO_PI_HI, in1=pr_th[:], op0=ALU.mult, op1=ALU.add)
        regroup_b(raw_bre, g_bre, 1)
        r2 = small("r2")
        nc.vector.scalar_tensor_tensor(out=r2[:], in0=ki[:], scalar=-TWO_PI_LO, in1=r1[:], op0=ALU.mult, op1=ALU.add)
        e1 = small("e1")
        nc.scalar.activation(out=e1[:], in_=pr_nu[:], func=ACTF.Exp)
        mag = small("mag")
        nc.scalar.activation(out=mag[:], in_=e1[:], func=ACTF.Exp, scale=-1.0)
        sa = small("sa")
        nc.scalar.activation(out=sa[:], in_=r2[:], func=ACTF.Sin, scale=0.5)
        sb = small("sb")
        nc.scalar.activation(out=sb[:], in_=r2[:], func=ACTF.Sin, scale=0.25)
        regroup_b(raw_bim, g_bim, 0)
        regroup_b(raw_bim, g_bim, 1)
        b_cd = [quant(g_bre[:], "bre")]
        gam = small("gam")
        nc.vector.tensor_copy(out=gam[:], in_=pr_ga[:])
        sam = small("sam")
        nc.vector.tensor_tensor(out=sam[:], in0=sa[:], in1=mag[:], op=ALU.mult)
        sb2 = small("sb2")
        nc.vector.tensor_tensor(out=sb2[:], in0=sb[:], in1=sb[:], op=ALU.mult)
        b_cd.append(quant(g_bim[:], "bim"))
        ss = small("ss")
        nc.vector.tensor_tensor(out=ss[:], in0=sa[:], in1=sam[:], op=ALU.mult)
        ch2 = small("ch2")
        nc.vector.tensor_scalar(out=ch2[:], in0=sb2[:], scalar1=-4.0, scalar2=2.0, op0=ALU.mult, op1=ALU.add)
        lam_re = small("lam_re")
        nc.vector.scalar_tensor_tensor(out=lam_re[:], in0=ss[:], scalar=-2.0, in1=mag[:], op0=ALU.mult, op1=ALU.add)
        lam_im = small("lam_im")
        nc.vector.tensor_tensor(out=lam_im[:], in0=sam[:], in1=ch2[:], op=ALU.mult)
        nlam_im = small("nlam_im")
        nc.vector.scalar_tensor_tensor(out=nlam_im[:], in0=sam[:], scalar=-1.0, in1=ch2[:], op0=ALU.mult, op1=ALU.mult)
        c_cd = []

        gu_t = {}
        ut_t = {}
        uq_t = {}
        du_t = {}
        xT_t = {}
        gx_t = {}
        xq_t = {}
        xo_t = {}
        yo_t = {}
        st_t = {}
        pp_t = {}
        xn_t = {}
        yy_t = {}

        g_c = work.tile([P, 2, 4 * WIDTH], BF16, tag="du", name="g_c", bufs=3, align_bytes=64)
        for ri, (raw, sign) in enumerate(((raw_cre, 1.0), (raw_cim, -1.0))):
            nc.gpsimd.tensor_scalar(
                out=g_c[:, ri, :].rearrange("p (n t) -> p n t", t=4),
                in0=raw[:].rearrange("p (t n) -> p n t", t=4),
                scalar1=sign, scalar2=0.0, op0=ALU.mult, op1=ALU.add,
            )

        def pe_ut(c, hc):
            u_w = u_t[c][:].bitcast(F32)
            ut = psum.tile([P, 2, 256], F32, tag="ut", name="ut")
            for jj in range(2):
                j = 2 * hc + jj
                for u in range(2):
                    nc.tensor.transpose(
                        ut[:, u, jj * P:(jj + 1) * P], u_w[:, j * 256 + u:(j + 1) * 256:2], ident[:]
                    )
            ut_t[(c, hc)] = ut

        def pe_sti(c, u):
            s_w = sim_t[c][:].bitcast(F32)
            st = psum.tile([P, rows(c)], F32, tag="sti", name="sti")
            for j in range(mt(c)):
                nc.tensor.transpose(st[:, j * P:(j + 1) * P], s_w[:, j * 256 + u:(j + 1) * 256:2], ident[:])
            st_t[(c, u, 1)] = st[:].bitcast(BF16).rearrange("p (m e) -> p e m", e=2)

        def pe_str(c, u):
            s_b = sre_t[c]
            st = psum.tile([P, 2, rows(c)], BF16, tag="str", name="str")
            for e in range(2):
                t = 2 * u + e
                for j in range(mt(c)):
                    nc.tensor.matmul(
                        st[:, e, j * P:(j + 1) * P], lhsT=s_b[:, j * WIDTH + t:(j + 1) * WIDTH:4], rhs=ident_b[:],
                        start=True, stop=True,
                    )
            st_t[(c, u, 0)] = st[:]

        def pe_m1(g):
            c, t = divmod(g, 4)
            uc, us = uq_t[c]
            for ri in range(2):
                cd, sc = b_cd[ri]
                pp = psum.tile([P, rows(c)], F32, tag="pp", name="pp", bufs=2)
                nc.tensor.matmul_mx(
                    out=pp[:],
                    lhsT=cd[:, t * P:(t + 1) * P].bitcast(FP8X4), lhsT_scale=sc[:, t * P:(t + 1) * P],
                    rhs=uc[:].bitcast(FP8X4), rhs_scale=us[:],
                    start=True, stop=True,
                )
                pp_t[(g, ri)] = pp

        def pe_xb(q):
            c, j = divmod(q, 4)
            if j >= mt(c):
                return
            for ri in range(2):
                xn = psum.tile([P, 4, P], F32, tag="xn", name="xn", bufs=2)
                for t in range(4):
                    nc.tensor.transpose(xn[:, t, :], xT_t[c][ri][:, t, j * P:(j + 1) * P], ident[:])
                xn_t[(q, ri)] = xn

        def pe_m2(yi, spare_banks):
            c, j = divmod(yi, 4)
            if j >= mt(c):
                return
            tg = "pp" if (spare_banks and yi % 3 != 0) else "yy"
            yy = psum.tile([P, WIDTH], F32, tag=tg, name="yy", bufs=(1 if tg == "yy" else 2))
            for ri in range(2):
                xc, xs = xq_t[(c, ri)]
                cd, sc = c_cd[ri]
                nc.tensor.matmul_mx(
                    out=yy[:],
                    lhsT=xc[:, j * P:(j + 1) * P].bitcast(FP8X4), lhsT_scale=xs[:, j * P:(j + 1) * P],
                    rhs=cd[:].bitcast(FP8X4), rhs_scale=sc[:],
                    start=(ri == 0), stop=(ri == 1),
                )
            yy_t[yi] = yy

        def act_ut(c, hc):
            if c not in gu_t:
                gu_t[c] = work.tile([P, 4 * rows(c)], BF16, tag="gu", name="gu", align_bytes=64)
            gu_w = gu_t[c][:].bitcast(F32).rearrange("p (m u) -> p m u", u=2)
            nc.scalar.copy(out=gu_w[:, hc * 256:(hc + 1) * 256, :], in_=ut_t[(c, hc)][:].rearrange("p u m -> p m u"))

        def act_a(g):
            c, t = divmod(g, 4)
            u, e = divmod(t, 2)
            if t == 0:
                xre = work.tile([P, 4, rows(c)], F32, tag="xTre", name="xTre", bufs=3)
                xim = work.tile([P, 4, rows(c)], F32, tag="xTim", name="xTim", bufs=3)
                xT_t[c] = (xre, xim)
            xre, xim = xT_t[c]
            s_re = st_t[(c, u, 0)]
            nc.scalar.activation(out=xre[:, t, :], in_=s_re[:, e, :], func=ACTF.Copy, scale=lam_re[:, t:t + 1])
            nc.scalar.activation(out=xim[:, t, :], in_=s_re[:, e, :], func=ACTF.Copy, scale=lam_im[:, t:t + 1])

        def act_xn(q):
            c, j = divmod(q, 4)
            if j == 0:
                xore = work.tile([P, mt(c), WIDTH], F32, tag="xore", name="xore")
                xoim = work.tile([P, mt(c), WIDTH], F32, tag="xoim", name="xoim")
                xo_t[c] = (xore, xoim)
            if j >= mt(c):
                return
            for ri in range(2):
                nc.scalar.copy(
                    out=xo_t[c][ri][:, j, :].rearrange("p (q t) -> p q t", t=4),
                    in_=xn_t[(q, ri)][:].rearrange("p t q -> p q t"),
                )

        def dve_b(g):
            c, t = divmod(g, 4)
            u, e = divmod(t, 2)
            xre, xim = xT_t[c]
            s_im = st_t[(c, u, 1)]
            nc.vector.scalar_tensor_tensor(
                out=xre[:, t, :], in0=s_im[:, e, :], scalar=nlam_im[:, t:t + 1], in1=xre[:, t, :],
                op0=ALU.mult, op1=ALU.add,
            )
            nc.vector.scalar_tensor_tensor(
                out=xim[:, t, :], in0=s_im[:, e, :], scalar=lam_re[:, t:t + 1], in1=xim[:, t, :],
                op0=ALU.mult, op1=ALU.add,
            )

        def dve_x(g):
            c, t = divmod(g, 4)
            for ri in range(2):
                x = xT_t[c][ri]
                nc.vector.scalar_tensor_tensor(
                    out=x[:, t, :], in0=pp_t[(g, ri)][:], scalar=gam[:, t:t + 1], in1=x[:, t, :],
                    op0=ALU.mult, op1=ALU.add,
                )

        def dve_qu(c):
            uc = work.tile([P, rows(c)], U32, tag="uc", name="uc", align_bytes=64)
            us = work.tile([P, rows(c)], U8, tag="us", name="us", align_bytes=64)
            nc.vector.quantize_mx(out=uc[:].bitcast(FP8X4), scales=us[:], in_=gu_t[c][:])
            uq_t[c] = (uc, us)

        def dve_qx(c, ri):
            tg = ("re", "im")[ri]
            xc = work.tile([P, rows(c)], U32, tag="xc" + tg, name="xc" + tg, align_bytes=64)
            xs = work.tile([P, rows(c)], U8, tag="xs" + tg, name="xs" + tg, align_bytes=64)
            nc.vector.quantize_mx(out=xc[:].bitcast(FP8X4), scales=xs[:], in_=gx_t[(c, ri)][:])
            xq_t[(c, ri)] = (xc, xs)

        def dve_y(yi):
            c, j = divmod(yi, 4)
            if j >= mt(c):
                return
            if j == 0:
                yo_t[c] = work.tile([P, mt(c), WIDTH], F32, tag="yo", name="yo", bufs=3)
            if mt(c) == 4 and j == Y_OFF:
                nc.scalar.copy(out=yo_t[c][:, j, :], in_=yy_t[yi][:])
                nc.gpsimd.tensor_tensor(out=yo_t[c][:, j, :], in0=yo_t[c][:, j, :], in1=du_t[c][:, j, :], op=ALU.add)
            else:
                nc.vector.tensor_tensor(out=yo_t[c][:, j, :], in0=yy_t[yi][:], in1=du_t[c][:, j, :], op=ALU.add)
            if j % 2 == 1:
                pair = slice(j - 1, j + 1)
                nc.sync.dma_start(
                    out=rows_of(out_0, c).rearrange("(i j) h -> i j h", j=mt(c))[:, pair, :], in_=yo_t[c][:, pair, :]
                )

        def pool_behind(codes):
            tok = work.tile([P, 1], U32, tag="tok", name="tok")
            nc.gpsimd.tensor_copy(out=tok[:], in_=codes[:, 0:1])

        def pool_du(c):
            du = work.tile([P, mt(c), WIDTH], F32, tag="du", name="du", bufs=3, align_bytes=64)
            nc.gpsimd.tensor_tensor(
                out=du[:],
                in0=u_t[c][:].rearrange("p (j k) -> p j k", j=mt(c)),
                in1=dbc[:].unsqueeze(1).to_broadcast([P, mt(c), WIDTH]),
                op=ALU.mult,
            )
            du_t[c] = du

        def cast_x(c, ri, engs):
            tg = ("gxre", "gxim")[ri]
            gx = work.tile([P, 4 * rows(c)], BF16, tag=tg, name=tg, align_bytes=64)
            part = rows(c) // len(engs)
            for i, eng in enumerate(engs):
                dst = gx[:, 4 * part * i:4 * part * (i + 1)].rearrange("p (m t) -> p m t", t=4)
                src = xT_t[c][ri][:, :, part * i:part * (i + 1)].rearrange("p t m -> p m t")
                if eng == "a":
                    nc.scalar.copy(out=dst, in_=src)
                elif eng == "v":
                    nc.vector.tensor_copy(out=dst, in_=src)
                else:
                    nc.gpsimd.tensor_scalar(out=dst, in0=src, scalar1=1.0, scalar2=0.0, op0=ALU.mult, op1=ALU.add)
            gx_t[(c, ri)] = gx

        def store(dram, c, src):
            nc.sync.dma_start(out=rows_of(dram, c).rearrange("(i j) h -> i j h", j=mt(c)), in_=src[:])

        def ut_at(g):
            c, k = divmod(g, 4)
            w = None
            if g in (-7, -5):
                w = (0, (g + 7) // 2)
            elif g in (0, 1):
                w = (1, g)
            elif c >= 0 and k >= 2 and ok(c + 2):
                w = (c + 2, k - 2)
            if w is not None and 2 * w[1] >= mt(w[0]):
                w = None
            return w

        for g in range(-8, NPL + YLAG):
            c, k = divmod(g, 4)
            if okp(g):
                dve_x(g)
            if okp(g - YLAG):
                dve_y(g - YLAG)
            if g == -4:
                dve_qu(0)
            if k == KQ:
                quantised = None
                if c >= 0 and ok(c + 1):
                    dve_qu(c + 1)
                    quantised = uq_t[c + 1][0]
                if c == 1:
                    c_cd.append(quant(g_c[:, 0, :], "cre"))
                    c_cd.append(quant(g_c[:, 1, :], "cim"))
                if ok(c - 1) and c - 1 != NCH - 1:
                    dve_qx(c - 1, 0)
                    dve_qx(c - 1, 1)
                    quantised = xq_t[(c - 1, 1)][0]
                if ok(c) and c != NCH - 1:
                    pool_behind(quantised)
                    pool_du(c)
            if g == NPL:
                dve_qx(NCH - 1, 0)
                dve_qx(NCH - 1, 1)
            if okp(g - 4):
                act_xn(g - 4)
            if ut_at(g) is not None:
                act_ut(ut_at(g)[0], ut_at(g)[1])
            if okp(g + 2):
                act_a(g + 2)
            if k == 3 and ok(c):
                cast_x(c, 0, "v" if c == NCH - 1 else "g")
                cast_x(c, 1, "va" if c == NCH - 1 else "ga")
                if c == NCH - 2:
                    pool_du(NCH - 1)
            if k == 2 and c >= 0:
                if ok(c + 3):
                    load_s(c + 3)
                if ok(c + 4):
                    load_u(c + 4)
            if k == 3 and ok(c - 1):
                store(out_1, c - 1, xo_t[c - 1][0])
                store(out_2, c - 1, xo_t[c - 1][1])
            if okp(g + 1) and (g + 1) % 2 == 0:
                pe_sti((g + 1) // 4, ((g + 1) % 4) // 2)
            if okp(g + 1):
                pe_m1(g + 1)
            if okp(g + 1 - YLAG):
                pe_m2(g + 1 - YLAG, g >= NPL - 1)
            if okp(g - 3):
                pe_xb(g - 3)
            if okp(g + 3) and (g + 3) % 2 == 0:
                pe_str((g + 3) // 4, ((g + 3) % 4) // 2)
            if ut_at(g + 1) is not None:
                pe_ut(ut_at(g + 1)[0], ut_at(g + 1)[1])
            if okp(g + 1):
                dve_b(g + 1)
